import numpy as np
import ml_dtypes


def mxq(x, axis, fmt="e4m3"):
    dtype, down = {"e4m3": (ml_dtypes.float8_e4m3fn, 7), "e5m2": (ml_dtypes.float8_e5m2, 14)}[fmt]
    v = np.moveaxis(np.asarray(x, np.float32).astype(ml_dtypes.bfloat16).astype(np.float64), axis, -1)
    blocks = v.reshape(v.shape[:-1] + (-1, 32))
    amax = np.abs(blocks).max(-1, keepdims=True)
    byte = np.maximum(np.where(amax > 0, np.frexp(amax)[1] - 1 + 127, 0) - down, 1)
    scale = np.exp2(byte - 127.0)
    codes = (blocks / scale).astype(np.float32).astype(dtype).astype(np.float64)
    return np.moveaxis((codes * scale).reshape(v.shape), -1, axis)


WIDE = False


def mx_kscale(k):
    if not WIDE:
        return np.ones(k)
    levels = np.array([10, -10, 5, -5, 0])
    a = np.random.permutation(np.resize(levels, k // 512 * 4)).reshape(k // 512, 4)
    idx = np.arange(k)
    return np.exp2(a[idx // 512, idx % 128 // 32])


BF16 = ml_dtypes.bfloat16


def bf(x):
    return np.asarray(x, np.float32).astype(BF16)


def f64(x):
    return np.asarray(x).astype(np.float64)


E2M1 = np.array([0.0, 0.5, 1.0, 1.5, 2.0, 3.0, 4.0, 6.0, -0.0, -0.5, -1.0, -1.5, -2.0, -3.0, -4.0, -6.0])


def pack_weight(w, fmt):
    k, n = w.shape
    w = f64(bf(w)).reshape(k // 32, 32, n)
    amax = np.abs(w).max(1)
    if fmt == "e4m3":
        byte = np.frexp(amax)[1] - 1 + 127 - 7
    else:
        mant, ex = np.frexp(amax / 6.0)
        byte = np.where(mant > 0.5, ex, ex - 1) + 127
    byte = np.clip(np.where(amax > 0, byte, 1), 1, 254)
    scaled = (w * np.exp2(127.0 - byte)[:, None, :]).reshape(k, n).astype(np.float32)
    by_word = np.ascontiguousarray(scaled.reshape(k // 512, 128, 4, n).transpose(0, 1, 3, 2))
    if fmt == "e4m3":
        words = by_word.astype(ml_dtypes.float8_e4m3fn).view(np.uint8)
    else:
        c = by_word.astype(ml_dtypes.float4_e2m1fn).view(np.uint8) & 0xF
        words = c[..., 0::2] | (c[..., 1::2] << 4)
    return np.ascontiguousarray(words), np.ascontiguousarray(byte.astype(np.uint8).reshape(k // 512, 16, n))


def unpack_weight(words, scales, fmt):
    g, p, n, _ = words.shape
    if fmt == "e4m3":
        vals = np.ascontiguousarray(words).view(ml_dtypes.float8_e4m3fn).astype(np.float64)
    else:
        nib = np.empty((g, p, n, 4), np.uint8)
        nib[..., 0::2] = words & 0xF
        nib[..., 1::2] = words >> 4
        vals = E2M1[nib]
    vals = vals * np.repeat(np.exp2(scales.astype(np.float64) - 127.0), 8, axis=1)[..., None]
    return vals.transpose(0, 1, 3, 2).reshape(g * 512, n)

def pack4(w):
    words, scales = pack_weight(w, "e2m1")
    return words.reshape(words.shape[0], 128, -1), scales


def unpack4(words, scales):
    return unpack_weight(words.reshape(words.shape[0], 128, -1, 2), scales, "e2m1")


B, IN, MEM, CTX, H, G = 512, 1024, 1024, 1024, 4, 3


def sigmoid(v):
    return 1.0 / (1.0 + np.exp(-v))


def setup_inputs():
    s = mx_kscale(IN)
    w = np.random.standard_normal((MEM, MEM + IN)) / np.sqrt(MEM + IN)
    w[:, MEM:] = w[:, MEM:] / s
    input_tensor = bf(np.random.standard_normal((B, IN)) * s)
    previous_memory = bf(np.random.standard_normal((B, MEM)))
    words, scales = pack4(np.ascontiguousarray(w.T))
    return {"input_tensor": input_tensor,
            "previous_memory": previous_memory,
            "fg_w_words": words,
            "fg_w_scales": scales,
            "fg_b": bf(np.random.standard_normal(MEM) * 0.3)}


def reference(input_tensor, previous_memory, fg_w_words, fg_w_scales, fg_b):
    m = f64(previous_memory)
    forget_in = np.concatenate([m, f64(input_tensor)], axis=-1)
    fgate = sigmoid((mxq(forget_in, 1, "e4m3") @ unpack4(fg_w_words, fg_w_scales)) + f64(fg_b))
    return m * fgate

@@ -1,0 +1,146 @@
+import concourse.mybir as mybir
+from concourse.masks import make_identity
+
+F32 = mybir.dt.float32
+BF16 = mybir.dt.bfloat16
+I32 = mybir.dt.int32
+U32 = mybir.dt.uint32
+U8 = mybir.dt.uint8
+FP8X4 = mybir.dt.float8_e4m3fn_x4
+FP4X4 = mybir.dt.float4_e2m1fn_x4
+ADD = mybir.AluOpType.add
+MULT = mybir.AluOpType.mult
+SIGMOID = mybir.ActivationFunctionType.Sigmoid
+
+P = 128
+PACK = 4
+K_PASS = P * PACK
+BATCH = 512
+MEM = 1024
+K = 2048
+ROW_TILES = BATCH // P
+PASSES = K // K_PASS
+N_TILE = 512
+N_TILES = MEM // N_TILE
+WORDS = K // 2
+PASS_WORDS = K_PASS // 2
+PASSES_PER_BANK = 2
+
+FLOPS = 2 * BATCH * K * MEM
+
+
+def tile_dynamicmemorycell_pa_kernel(
+    tc, input_tensor, previous_memory, fg_w_words, fg_w_scales, fg_b, out
+):
+    nc = tc.nc
+    with tc.tile_pool(name="keep", bufs=1) as keep, tc.tile_pool(
+        name="stage", bufs=ROW_TILES
+    ) as stage, tc.tile_pool(name="work", bufs=4) as work, tc.psum_pool(
+        name="flip", bufs=4
+    ) as flip, tc.psum_pool(name="sums", bufs=4) as sums:
+        forget_in = [
+            keep.tile([P, K], BF16, name="forget_in%d" % i) for i in range(ROW_TILES)
+        ]
+        x_codes = keep.tile([P, ROW_TILES, PASSES * P], U32, align_bytes=64)
+        x_scales = keep.tile([P, ROW_TILES, PASSES * P], U8, align_bytes=64)
+        w_codes = keep.tile([P, N_TILES, PASSES, 2 * N_TILE], U8, align_bytes=64)
+        w_scales = keep.tile([P, PASSES, MEM], U8, align_bytes=64)
+        identity = keep.tile([P, P], F32)
+        ones = keep.tile([P, P], BF16)
+        bias_rows = keep.tile([P, MEM], BF16)
+        bias_all = keep.tile([P, MEM], F32)
+        table_warm = keep.tile([P, 1], F32)
+
+        nc.vector.memset(w_scales[:].bitcast(I32), 0)
+        nc.vector.memset(bias_rows[:], 0.0)
+        nc.vector.memset(ones[:], 1.0)
+        nc.vector.memset(table_warm[:], 0.0)
+        make_identity(nc, identity[:])
+        nc.scalar.activation(out=table_warm[:], in_=table_warm[:], func=SIGMOID)
+
+        def load_rows(i):
+            rows = slice(i * P, (i + 1) * P)
+            nc.sync.dma_start(out=forget_in[i][:, 0:MEM], in_=previous_memory[rows, :])
+            nc.sync.dma_start(out=forget_in[i][:, MEM:K], in_=input_tensor[rows, :])
+
+        nc.scalar.dma_start(
+            out=bias_rows[0:1, :], in_=fg_b.rearrange("(o n) -> o n", o=1)
+        )
+        load_rows(0)
+        load_rows(1)
+        scale_rows = fg_w_scales.rearrange("g (q r) n -> r q g n", r=4)
+        for r in range(4):
+            nc.sync.dma_start(
+                out=w_scales[r:P:32, :, :].bitcast(I32), in_=scale_rows[r].bitcast(I32)
+            )
+        load_rows(2)
+        load_rows(3)
+        for h in range(N_TILES):
+            nc.sync.dma_start(
+                out=w_codes[:, h, :, :].bitcast(I32),
+                in_=fg_w_words[:, :, h * 2 * N_TILE : (h + 1) * 2 * N_TILE]
+                .rearrange("g p c -> p g c")
+                .bitcast(I32),
+            )
+
+        for h in range(N_TILES):
+            cols = slice(h * N_TILE, (h + 1) * N_TILE)
+            bias_sum = sums.tile([P, N_TILE], F32, tag="sum")
+            nc.tensor.matmul(
+                out=bias_sum[:], lhsT=ones[:], rhs=bias_rows[:, cols], start=True, stop=True
+            )
+            nc.scalar.copy(out=bias_all[:, cols], in_=bias_sum[:])
+
+        for i in range(ROW_TILES):
+            words = forget_in[i][:].bitcast(F32)
+            grouped = stage.tile([P, PASSES * P * PACK], BF16, align_bytes=64)
+            grouped_words = grouped[:].bitcast(F32).rearrange(
+                "p (g b u) -> p g b u", g=PASSES, u=2
+            )
+            for half in range(PASSES // PASSES_PER_BANK):
+                flipped = flip.tile([P, PASSES_PER_BANK * 2, P], F32)
+                for j in range(PASSES_PER_BANK):
+                    g = half * PASSES_PER_BANK + j
+                    for u in range(2):
+                        nc.tensor.transpose(
+                            flipped[:, 2 * j + u, :],
+                            words[:, g * PASS_WORDS + u : (g + 1) * PASS_WORDS : 2],
+                            identity[:],
+                        )
+                copy = nc.scalar.copy if half % 2 == 0 else nc.vector.tensor_copy
+                copy(
+                    out=grouped_words[
+                        :, half * PASSES_PER_BANK : (half + 1) * PASSES_PER_BANK, :, :
+                    ],
+                    in_=flipped[:].rearrange("p (g u) b -> p g b u", u=2),
+                )
+            nc.vector.quantize_mx(
+                out=x_codes[:, i, :].bitcast(FP8X4), scales=x_scales[:, i, :], in_=grouped[:]
+            )
+
+        for h in range(N_TILES):
+            cols = slice(h * N_TILE, (h + 1) * N_TILE)
+            for i in range(ROW_TILES):
+                total = sums.tile([P, N_TILE], F32, tag="sum")
+                for g in range(PASSES):
+                    batch = slice(g * P, (g + 1) * P)
+                    nc.tensor.matmul_mx(
+                        out=total[:],
+                        lhsT=x_codes[:, i, batch].bitcast(FP8X4),
+                        lhsT_scale=x_scales[:, i, batch],
+                        rhs=w_codes[:, h, g, :].bitcast(FP4X4),
+                        rhs_scale=w_scales[:, g, cols],
+                        start=(g == 0),
+                        stop=(g == PASSES - 1),
+                    )
+                logit = work.tile([P, N_TILE], F32)
+                nc.vector.tensor_tensor(
+                    out=logit[:], in0=total[:], in1=bias_all[:, cols], op=ADD
+                )
+                gate = work.tile([P, N_TILE], F32)
+                nc.scalar.activation(out=gate[:], in_=logit[:], func=SIGMOID)
+                result = work.tile([P, N_TILE], F32)
+                nc.vector.tensor_tensor(
+                    out=result[:], in0=gate[:], in1=forget_in[i][:, cols], op=MULT
+                )
+                nc.sync.dma_start(out=out[i * P : (i + 1) * P, cols], in_=result[:])

@@ -17,34 +17,40 @@ PACK = 4
 K_PASS = P * PACK
 BATCH = 512
 MEM = 1024
-K = 2048
-ROW_TILES = BATCH // P
-PASSES = K // K_PASS
+SOURCES = 2
+PASSES = MEM // K_PASS
+PAIRS = 2
+TWINS = 2
 N_TILE = 512
 N_TILES = MEM // N_TILE
-WORDS = K // 2
 PASS_WORDS = K_PASS // 2
-PASSES_PER_BANK = 2
 
-FLOPS = 2 * BATCH * K * MEM
+FLOPS = 2 * BATCH * SOURCES * MEM * MEM
 
 
 def tile_dynamicmemorycell_pa_kernel(
     tc, input_tensor, previous_memory, fg_w_words, fg_w_scales, fg_b, out
 ):
     nc = tc.nc
+    sources = [
+        source.rearrange("(a p t) c -> a p t c", p=P, t=TWINS)
+        for source in (previous_memory, input_tensor)
+    ]
+    out_tiles = out.rearrange("(a p t) c -> a t p c", p=P, t=TWINS)
+
     with tc.tile_pool(name="keep", bufs=1) as keep, tc.tile_pool(
-        name="stage", bufs=ROW_TILES
+        name="stage", bufs=4
     ) as stage, tc.tile_pool(name="work", bufs=4) as work, tc.psum_pool(
         name="flip", bufs=4
-    ) as flip, tc.psum_pool(name="sums", bufs=4) as sums:
+    ) as flip, tc.psum_pool(name="sums", bufs=4) as sums, tc.manual_schedule():
         forget_in = [
-            keep.tile([P, K], BF16, name="forget_in%d" % i) for i in range(ROW_TILES)
+            keep.tile([P, SOURCES, TWINS, MEM], BF16, name="forget_in%d" % a)
+            for a in range(PAIRS)
         ]
-        x_codes = keep.tile([P, ROW_TILES, PASSES * P], U32, align_bytes=64)
-        x_scales = keep.tile([P, ROW_TILES, PASSES * P], U8, align_bytes=64)
-        w_codes = keep.tile([P, N_TILES, PASSES, 2 * N_TILE], U8, align_bytes=64)
-        w_scales = keep.tile([P, PASSES, MEM], U8, align_bytes=64)
+        x_codes = keep.tile([P, PAIRS, TWINS, SOURCES, PASSES * P], U32, align_bytes=64)
+        x_scales = keep.tile([P, PAIRS, TWINS, SOURCES, PASSES * P], U8, align_bytes=64)
+        w_codes = keep.tile([P, N_TILES, SOURCES * PASSES, 2 * N_TILE], U8, align_bytes=64)
+        w_scales = keep.tile([P, SOURCES * PASSES, MEM], U8, align_bytes=64)
         identity = keep.tile([P, P], F32)
         ones = keep.tile([P, P], BF16)
         bias_rows = keep.tile([P, MEM], BF16)
@@ -58,23 +64,18 @@ def tile_dynamicmemorycell_pa_kernel(
         make_identity(nc, identity[:])
         nc.scalar.activation(out=table_warm[:], in_=table_warm[:], func=SIGMOID)
 
-        def load_rows(i):
-            rows = slice(i * P, (i + 1) * P)
-            nc.sync.dma_start(out=forget_in[i][:, 0:MEM], in_=previous_memory[rows, :])
-            nc.sync.dma_start(out=forget_in[i][:, MEM:K], in_=input_tensor[rows, :])
+        def load_pair(a):
+            for s in range(SOURCES):
+                nc.sync.dma_start(out=forget_in[a][:, s, :, :], in_=sources[s][a])
 
-        nc.scalar.dma_start(
-            out=bias_rows[0:1, :], in_=fg_b.rearrange("(o n) -> o n", o=1)
-        )
-        load_rows(0)
-        load_rows(1)
+        load_pair(0)
         scale_rows = fg_w_scales.rearrange("g (q r) n -> r q g n", r=4)
         for r in range(4):
             nc.sync.dma_start(
                 out=w_scales[r:P:32, :, :].bitcast(I32), in_=scale_rows[r].bitcast(I32)
             )
-        load_rows(2)
-        load_rows(3)
+        nc.sync.dma_start(out=bias_rows[0:1, :], in_=fg_b.rearrange("(o n) -> o n", o=1))
+        load_pair(1)
         for h in range(N_TILES):
             nc.sync.dma_start(
                 out=w_codes[:, h, :, :].bitcast(I32),
@@ -82,6 +83,35 @@ def tile_dynamicmemorycell_pa_kernel(
                 .rearrange("g p c -> p g c")
                 .bitcast(I32),
             )
+
+        for a in range(PAIRS):
+            for s in range(SOURCES):
+                grouped = []
+                for t in range(TWINS):
+                    words = forget_in[a][:, s, t, :].bitcast(F32)
+                    flipped = flip.tile([P, PASSES, 2, P], F32)
+                    for g in range(PASSES):
+                        for u in range(2):
+                            nc.tensor.transpose(
+                                flipped[:, g, u, :],
+                                words[:, g * PASS_WORDS + u : (g + 1) * PASS_WORDS : 2],
+                                identity[:],
+                            )
+                    side_by_side = stage.tile([P, PASSES * P * PACK], BF16, align_bytes=64)
+                    copy = nc.scalar.copy if t % 2 == 0 else nc.vector.tensor_copy
+                    copy(
+                        out=side_by_side[:]
+                        .bitcast(F32)
+                        .rearrange("p (g b u) -> p g b u", g=PASSES, u=2),
+                        in_=flipped[:].rearrange("p g u b -> p g b u"),
+                    )
+                    grouped.append(side_by_side)
+                for t in range(TWINS):
+                    nc.vector.quantize_mx(
+                        out=x_codes[:, a, t, s, :].bitcast(FP8X4),
+                        scales=x_scales[:, a, t, s, :],
+                        in_=grouped[t][:],
+                    )
 
         for h in range(N_TILES):
             cols = slice(h * N_TILE, (h + 1) * N_TILE)
@@ -91,56 +121,39 @@ def tile_dynamicmemorycell_pa_kernel(
             )
             nc.scalar.copy(out=bias_all[:, cols], in_=bias_sum[:])
 
-        for i in range(ROW_TILES):
-            words = forget_in[i][:].bitcast(F32)
-            grouped = stage.tile([P, PASSES * P * PACK], BF16, align_bytes=64)
-            grouped_words = grouped[:].bitcast(F32).rearrange(
-                "p (g b u) -> p g b u", g=PASSES, u=2
-            )
-            for half in range(PASSES // PASSES_PER_BANK):
-                flipped = flip.tile([P, PASSES_PER_BANK * 2, P], F32)
-                for j in range(PASSES_PER_BANK):
-                    g = half * PASSES_PER_BANK + j
-                    for u in range(2):
-                        nc.tensor.transpose(
-                            flipped[:, 2 * j + u, :],
-                            words[:, g * PASS_WORDS + u : (g + 1) * PASS_WORDS : 2],
-                            identity[:],
-                        )
-                copy = nc.scalar.copy if half % 2 == 0 else nc.vector.tensor_copy
-                copy(
-                    out=grouped_words[
-                        :, half * PASSES_PER_BANK : (half + 1) * PASSES_PER_BANK, :, :
-                    ],
-                    in_=flipped[:].rearrange("p (g u) b -> p g b u", u=2),
-                )
-            nc.vector.quantize_mx(
-                out=x_codes[:, i, :].bitcast(FP8X4), scales=x_scales[:, i, :], in_=grouped[:]
-            )
-
-        for h in range(N_TILES):
+        def gate_of(h, a, t):
             cols = slice(h * N_TILE, (h + 1) * N_TILE)
-            for i in range(ROW_TILES):
-                total = sums.tile([P, N_TILE], F32, tag="sum")
+            total = sums.tile([P, N_TILE], F32, tag="sum")
+            for s in range(SOURCES):
                 for g in range(PASSES):
                     batch = slice(g * P, (g + 1) * P)
                     nc.tensor.matmul_mx(
                         out=total[:],
-                        lhsT=x_codes[:, i, batch].bitcast(FP8X4),
-                        lhsT_scale=x_scales[:, i, batch],
-                        rhs=w_codes[:, h, g, :].bitcast(FP4X4),
-                        rhs_scale=w_scales[:, g, cols],
-                        start=(g == 0),
-                        stop=(g == PASSES - 1),
+                        lhsT=x_codes[:, a, t, s, batch].bitcast(FP8X4),
+                        lhsT_scale=x_scales[:, a, t, s, batch],
+                        rhs=w_codes[:, h, s * PASSES + g, :].bitcast(FP4X4),
+                        rhs_scale=w_scales[:, s * PASSES + g, cols],
+                        start=(s == 0 and g == 0),
+                        stop=(s == SOURCES - 1 and g == PASSES - 1),
                     )
-                logit = work.tile([P, N_TILE], F32)
-                nc.vector.tensor_tensor(
-                    out=logit[:], in0=total[:], in1=bias_all[:, cols], op=ADD
-                )
-                gate = work.tile([P, N_TILE], F32)
-                nc.scalar.activation(out=gate[:], in_=logit[:], func=SIGMOID)
-                result = work.tile([P, N_TILE], F32)
-                nc.vector.tensor_tensor(
-                    out=result[:], in0=gate[:], in1=forget_in[i][:, cols], op=MULT
-                )
-                nc.sync.dma_start(out=out[i * P : (i + 1) * P, cols], in_=result[:])
+            logit = work.tile([P, N_TILE], F32)
+            nc.vector.tensor_tensor(out=logit[:], in0=total[:], in1=bias_all[:, cols], op=ADD)
+            gate = work.tile([P, N_TILE], F32)
+            nc.scalar.activation(out=gate[:], in_=logit[:], func=SIGMOID)
+            return gate
+
+        def store_gated(gate, h, a, t):
+            cols = slice(h * N_TILE, (h + 1) * N_TILE)
+            result = work.tile([P, N_TILE], F32)
+            nc.vector.tensor_tensor(
+                out=result[:], in0=gate[:], in1=forget_in[a][:, 0, t, cols], op=MULT
+            )
+            nc.sync.dma_start(out=out_tiles[a][t][:, cols], in_=result[:])
+
+        banks = [(h, a, t) for h in range(N_TILES) for a in range(PAIRS) for t in range(TWINS)]
+        gates = []
+        for j in range(len(banks)):
+            gates.append(gate_of(*banks[j]))
+            if j > 0:
+                store_gated(gates[j - 1], *banks[j - 1])
+        store_gated(gates[-1], *banks[-1])

@@ -145,9 +145,8 @@ def tile_dynamicmemorycell_pa_kernel(
         def store_gated(gate, h, a, t):
             cols = slice(h * N_TILE, (h + 1) * N_TILE)
             result = work.tile([P, N_TILE], F32)
-            nc.vector.tensor_tensor(
-                out=result[:], in0=gate[:], in1=forget_in[a][:, 0, t, cols], op=MULT
-            )
+            multiply = nc.gpsimd.tensor_tensor if t % 2 == 0 else nc.vector.tensor_tensor
+            multiply(out=result[:], in0=gate[:], in1=forget_in[a][:, 0, t, cols], op=MULT)
             nc.sync.dma_start(out=out_tiles[a][t][:, cols], in_=result[:])
 
         banks = [(h, a, t) for h in range(N_TILES) for a in range(PAIRS) for t in range(TWINS)]

@@ -23,6 +23,7 @@ PAIRS = 2
 TWINS = 2
 N_TILE = 512
 N_TILES = MEM // N_TILE
+N_GROUP = 128
 PASS_WORDS = K_PASS // 2
 
 FLOPS = 2 * BATCH * SOURCES * MEM * MEM
@@ -89,7 +90,7 @@ def tile_dynamicmemorycell_pa_kernel(
                 grouped = []
                 for t in range(TWINS):
                     words = forget_in[a][:, s, t, :].bitcast(F32)
-                    flipped = flip.tile([P, PASSES, 2, P], F32)
+                    flipped = flip.tile([P, PASSES, 2, P], F32, tag="flipped")
                     for g in range(PASSES):
                         for u in range(2):
                             nc.tensor.transpose(
@@ -136,23 +137,77 @@ def tile_dynamicmemorycell_pa_kernel(
                         start=(s == 0 and g == 0),
                         stop=(s == SOURCES - 1 and g == PASSES - 1),
                     )
-            logit = work.tile([P, N_TILE], F32)
+            logit = work.tile([P, N_TILE], F32, tag="logit")
             nc.vector.tensor_tensor(out=logit[:], in0=total[:], in1=bias_all[:, cols], op=ADD)
-            gate = work.tile([P, N_TILE], F32)
+            gate = work.tile([P, N_TILE], F32, tag="gate")
             nc.scalar.activation(out=gate[:], in_=logit[:], func=SIGMOID)
             return gate
 
-        def store_gated(gate, h, a, t):
+        def store_gated(gate, h, a, t, engine):
             cols = slice(h * N_TILE, (h + 1) * N_TILE)
-            result = work.tile([P, N_TILE], F32)
-            multiply = nc.gpsimd.tensor_tensor if t % 2 == 0 else nc.vector.tensor_tensor
-            multiply(out=result[:], in0=gate[:], in1=forget_in[a][:, 0, t, cols], op=MULT)
+            result = work.tile([P, N_TILE], F32, tag="result")
+            engine.tensor_tensor(
+                out=result[:], in0=gate[:], in1=forget_in[a][:, 0, t, cols], op=MULT
+            )
             nc.sync.dma_start(out=out_tiles[a][t][:, cols], in_=result[:])
 
         banks = [(h, a, t) for h in range(N_TILES) for a in range(PAIRS) for t in range(TWINS)]
         gates = []
-        for j in range(len(banks)):
+        for j in range(len(banks) - 1):
             gates.append(gate_of(*banks[j]))
-            if j > 0:
-                store_gated(gates[j - 1], *banks[j - 1])
-        store_gated(gates[-1], *banks[-1])
+            if 0 < j < len(banks) - 2:
+                store_gated(gates[j - 1], *banks[j - 1], nc.gpsimd if j % 2 == 1 else nc.vector)
+
+        h_last, a_last, t_last = banks[-1]
+        logit_last = work.tile([P, N_TILE], F32, tag="logit")
+        gate_last = work.tile([P, N_TILE], F32, tag="gate")
+        result_last = work.tile([P, N_TILE], F32, tag="result")
+
+        def logit_of_group(c):
+            inner = slice(c * N_GROUP, (c + 1) * N_GROUP)
+            cols = slice(h_last * N_TILE + c * N_GROUP, h_last * N_TILE + (c + 1) * N_GROUP)
+            bank = flip.tile([P, PASSES, 2, P], F32, tag="flipped")
+            total = bank[:, 0, 0, :]
+            for s in range(SOURCES):
+                for g in range(PASSES):
+                    batch = slice(g * P, (g + 1) * P)
+                    nc.tensor.matmul_mx(
+                        out=total,
+                        lhsT=x_codes[:, a_last, t_last, s, batch].bitcast(FP8X4),
+                        lhsT_scale=x_scales[:, a_last, t_last, s, batch],
+                        rhs=w_codes[
+                            :, h_last, s * PASSES + g, 2 * c * N_GROUP : 2 * (c + 1) * N_GROUP
+                        ].bitcast(FP4X4),
+                        rhs_scale=w_scales[:, s * PASSES + g, cols],
+                        start=(s == 0 and g == 0),
+                        stop=(s == SOURCES - 1 and g == PASSES - 1),
+                    )
+            nc.vector.tensor_tensor(
+                out=logit_last[:, inner], in0=total, in1=bias_all[:, cols], op=ADD
+            )
+
+        def gate_of_half(d):
+            inner = slice(d * 2 * N_GROUP, (d + 1) * 2 * N_GROUP)
+            nc.scalar.activation(out=gate_last[:, inner], in_=logit_last[:, inner], func=SIGMOID)
+
+        def store_gated_half(d):
+            inner = slice(d * 2 * N_GROUP, (d + 1) * 2 * N_GROUP)
+            cols = slice(h_last * N_TILE + d * 2 * N_GROUP, h_last * N_TILE + (d + 1) * 2 * N_GROUP)
+            nc.vector.tensor_tensor(
+                out=result_last[:, inner],
+                in0=gate_last[:, inner],
+                in1=forget_in[a_last][:, 0, t_last, cols],
+                op=MULT,
+            )
+            nc.sync.dma_start(out=out_tiles[a_last][t_last][:, cols], in_=result_last[:, inner])
+
+        logit_of_group(0)
+        logit_of_group(1)
+        gate_of_half(0)
+        logit_of_group(2)
+        logit_of_group(3)
+        gate_of_half(1)
+        store_gated(gates[-2], *banks[-3], nc.gpsimd)
+        store_gated(gates[-1], *banks[-2], nc.vector)
+        store_gated_half(0)
+        store_gated_half(1)

@@ -23,6 +23,7 @@ PAIRS = 2
 TWINS = 2
 N_TILE = 512
 N_TILES = MEM // N_TILE
+WARM_UPS = 4
 N_GROUP = 128
 PASS_WORDS = K_PASS // 2
 
@@ -57,7 +58,9 @@ def tile_dynamicmemorycell_pa_kernel(
         bias_rows = keep.tile([P, MEM], BF16)
         bias_all = keep.tile([P, MEM], F32)
         table_warm = keep.tile([P, 1], F32)
+        clock_warm = keep.tile([P, N_TILE], BF16)
 
+        nc.gpsimd.memset(clock_warm[:].bitcast(F32), 0.0)
         nc.vector.memset(w_scales[:].bitcast(I32), 0)
         nc.vector.memset(bias_rows[:], 0.0)
         nc.vector.memset(ones[:], 1.0)
@@ -84,6 +87,24 @@ def tile_dynamicmemorycell_pa_kernel(
                 .rearrange("g p c -> p g c")
                 .bitcast(I32),
             )
+
+        idle_sum = sums.tile([P, N_TILE], F32, tag="sum")
+
+        def idle_product():
+            nc.tensor.matmul(
+                out=idle_sum[:], lhsT=clock_warm[:, 0:P], rhs=clock_warm[:], start=True, stop=True
+            )
+
+        def spread_bias(h):
+            cols = slice(h * N_TILE, (h + 1) * N_TILE)
+            bias_sum = sums.tile([P, N_TILE], F32, tag="sum")
+            nc.tensor.matmul(
+                out=bias_sum[:], lhsT=ones[:], rhs=bias_rows[:, cols], start=True, stop=True
+            )
+            nc.scalar.copy(out=bias_all[:, cols], in_=bias_sum[:])
+
+        for i in range(WARM_UPS):
+            idle_product()
 
         for a in range(PAIRS):
             for s in range(SOURCES):
@@ -113,14 +134,10 @@ def tile_dynamicmemorycell_pa_kernel(
                         scales=x_scales[:, a, t, s, :],
                         in_=grouped[t][:],
                     )
-
-        for h in range(N_TILES):
-            cols = slice(h * N_TILE, (h + 1) * N_TILE)
-            bias_sum = sums.tile([P, N_TILE], F32, tag="sum")
-            nc.tensor.matmul(
-                out=bias_sum[:], lhsT=ones[:], rhs=bias_rows[:, cols], start=True, stop=True
-            )
-            nc.scalar.copy(out=bias_all[:, cols], in_=bias_sum[:])
+                if a == 0 and s == 0:
+                    idle_product()
+                elif a == 0 or s == 0:
+                    spread_bias(a)
 
         def gate_of(h, a, t):
             cols = slice(h * N_TILE, (h + 1) * N_TILE)

@@ -80,13 +80,19 @@ def tile_dynamicmemorycell_pa_kernel(
             )
         nc.sync.dma_start(out=bias_rows[0:1, :], in_=fg_b.rearrange("(o n) -> o n", o=1))
         load_pair(1)
-        for h in range(N_TILES):
+        def load_w_codes(h, first_pass, passes):
             nc.sync.dma_start(
-                out=w_codes[:, h, :, :].bitcast(I32),
-                in_=fg_w_words[:, :, h * 2 * N_TILE : (h + 1) * 2 * N_TILE]
+                out=w_codes[:, h, first_pass : first_pass + passes, :].bitcast(I32),
+                in_=fg_w_words[
+                    first_pass : first_pass + passes, :, h * 2 * N_TILE : (h + 1) * 2 * N_TILE
+                ]
                 .rearrange("g p c -> p g c")
                 .bitcast(I32),
             )
+
+        for s in range(SOURCES):
+            load_w_codes(0, s * PASSES, PASSES)
+        load_w_codes(1, 0, SOURCES * PASSES)
 
         idle_sum = sums.tile([P, N_TILE], F32, tag="sum")
 

@@ -70,7 +70,13 @@ def tile_dynamicmemorycell_pa_kernel(
 
         def load_pair(a):
             for s in range(SOURCES):
-                nc.sync.dma_start(out=forget_in[a][:, s, :, :], in_=sources[s][a])
+                if a == PAIRS - 1 and s == SOURCES - 1:
+                    for t in range(TWINS):
+                        nc.sync.dma_start(
+                            out=forget_in[a][:, s, t, :], in_=sources[s][a][:, t, :]
+                        )
+                else:
+                    nc.sync.dma_start(out=forget_in[a][:, s, :, :], in_=sources[s][a])
 
         load_pair(0)
         scale_rows = fg_w_scales.rearrange("g (q r) n -> r q g n", r=4)

@@ -146,9 +146,7 @@ def tile_dynamicmemorycell_pa_kernel(
                         scales=x_scales[:, a, t, s, :],
                         in_=grouped[t][:],
                     )
-                if a == 0 and s == 0:
-                    idle_product()
-                elif a == 0 or s == 0:
+                if a + s == 1:
                     spread_bias(a)
 
         def gate_of(h, a, t):

@@ -80,10 +80,16 @@ def tile_dynamicmemorycell_pa_kernel(
 
         load_pair(0)
         scale_rows = fg_w_scales.rearrange("g (q r) n -> r q g n", r=4)
-        for r in range(4):
-            nc.sync.dma_start(
-                out=w_scales[r:P:32, :, :].bitcast(I32), in_=scale_rows[r].bitcast(I32)
-            )
+
+        def load_w_scales(h):
+            cols = slice(h * N_TILE, (h + 1) * N_TILE)
+            for r in range(4):
+                nc.sync.dma_start(
+                    out=w_scales[r:P:32, :, cols].bitcast(I32),
+                    in_=scale_rows[r][:, :, cols].bitcast(I32),
+                )
+
+        load_w_scales(0)
         nc.sync.dma_start(out=bias_rows[0:1, :], in_=fg_b.rearrange("(o n) -> o n", o=1))
         load_pair(1)
         def load_w_codes(h, first_pass, passes):
@@ -98,6 +104,7 @@ def tile_dynamicmemorycell_pa_kernel(
 
         for s in range(SOURCES):
             load_w_codes(0, s * PASSES, PASSES)
+        load_w_scales(1)
         load_w_codes(1, 0, SOURCES * PASSES)
 
         idle_sum = sums.tile([P, N_TILE], F32, tag="sum")

@@ -104,8 +104,8 @@ def tile_dynamicmemorycell_pa_kernel(
 
         for s in range(SOURCES):
             load_w_codes(0, s * PASSES, PASSES)
-        load_w_scales(1)
         load_w_codes(1, 0, SOURCES * PASSES)
+        load_w_scales(1)
 
         idle_sum = sums.tile([P, N_TILE], F32, tag="sum")
 

@@ -52,7 +52,10 @@ def tile_dynamicmemorycell_pa_kernel(
         x_codes = keep.tile([P, PAIRS, TWINS, SOURCES, PASSES * P], U32, align_bytes=64)
         x_scales = keep.tile([P, PAIRS, TWINS, SOURCES, PASSES * P], U8, align_bytes=64)
         w_codes = keep.tile([P, N_TILES, SOURCES * PASSES, 2 * N_TILE], U8, align_bytes=64)
-        w_scales = keep.tile([P, SOURCES * PASSES, MEM], U8, align_bytes=64)
+        w_scales = [
+            keep.tile([P, SOURCES * PASSES, N_TILE], U8, align_bytes=64, name="w_scales%d" % h)
+            for h in range(N_TILES)
+        ]
         identity = keep.tile([P, P], F32)
         ones = keep.tile([P, P], BF16)
         bias_rows = keep.tile([P, MEM], BF16)
@@ -61,7 +64,8 @@ def tile_dynamicmemorycell_pa_kernel(
         clock_warm = keep.tile([P, N_TILE], BF16)
 
         nc.gpsimd.memset(clock_warm[:].bitcast(F32), 0.0)
-        nc.vector.memset(w_scales[:].bitcast(I32), 0)
+        for h in range(N_TILES):
+            nc.vector.memset(w_scales[h][:].bitcast(I32), 0)
         nc.vector.memset(bias_rows[:], 0.0)
         nc.vector.memset(ones[:], 1.0)
         nc.vector.memset(table_warm[:], 0.0)
@@ -85,7 +89,7 @@ def tile_dynamicmemorycell_pa_kernel(
             cols = slice(h * N_TILE, (h + 1) * N_TILE)
             for r in range(4):
                 nc.sync.dma_start(
-                    out=w_scales[r:P:32, :, cols].bitcast(I32),
+                    out=w_scales[h][r:P:32, :, :].bitcast(I32),
                     in_=scale_rows[r][:, :, cols].bitcast(I32),
                 )
 
@@ -104,8 +108,8 @@ def tile_dynamicmemorycell_pa_kernel(
 
         for s in range(SOURCES):
             load_w_codes(0, s * PASSES, PASSES)
-        load_w_codes(1, 0, SOURCES * PASSES)
         load_w_scales(1)
+        load_w_codes(1, 0, SOURCES * PASSES)
 
         idle_sum = sums.tile([P, N_TILE], F32, tag="sum")
 
@@ -167,7 +171,7 @@ def tile_dynamicmemorycell_pa_kernel(
                         lhsT=x_codes[:, a, t, s, batch].bitcast(FP8X4),
                         lhsT_scale=x_scales[:, a, t, s, batch],
                         rhs=w_codes[:, h, s * PASSES + g, :].bitcast(FP4X4),
-                        rhs_scale=w_scales[:, s * PASSES + g, cols],
+                        rhs_scale=w_scales[h][:, s * PASSES + g, :],
                         start=(s == 0 and g == 0),
                         stop=(s == SOURCES - 1 and g == PASSES - 1),
                     )
@@ -212,7 +216,7 @@ def tile_dynamicmemorycell_pa_kernel(
                         rhs=w_codes[
                             :, h_last, s * PASSES + g, 2 * c * N_GROUP : 2 * (c + 1) * N_GROUP
                         ].bitcast(FP4X4),
-                        rhs_scale=w_scales[:, s * PASSES + g, cols],
+                        rhs_scale=w_scales[h_last][:, s * PASSES + g, inner],
                         start=(s == 0 and g == 0),
                         stop=(s == SOURCES - 1 and g == PASSES - 1),
                     )

import concourse.mybir as mybir
from concourse.masks import make_identity

F32 = mybir.dt.float32
BF16 = mybir.dt.bfloat16
I32 = mybir.dt.int32
U32 = mybir.dt.uint32
U8 = mybir.dt.uint8
FP8X4 = mybir.dt.float8_e4m3fn_x4
FP4X4 = mybir.dt.float4_e2m1fn_x4
ADD = mybir.AluOpType.add
MULT = mybir.AluOpType.mult
SIGMOID = mybir.ActivationFunctionType.Sigmoid

P = 128
PACK = 4
K_PASS = P * PACK
BATCH = 512
MEM = 1024
SOURCES = 2
PASSES = MEM // K_PASS
PAIRS = 2
TWINS = 2
N_TILE = 512
N_TILES = MEM // N_TILE
WARM_UPS = 4
N_GROUP = 128
PASS_WORDS = K_PASS // 2

FLOPS = 2 * BATCH * SOURCES * MEM * MEM


def tile_dynamicmemorycell_pa_kernel(
    tc, input_tensor, previous_memory, fg_w_words, fg_w_scales, fg_b, out
):
    nc = tc.nc
    sources = [
        source.rearrange("(a p t) c -> a p t c", p=P, t=TWINS)
        for source in (previous_memory, input_tensor)
    ]
    out_tiles = out.rearrange("(a p t) c -> a t p c", p=P, t=TWINS)

    with tc.tile_pool(name="keep", bufs=1) as keep, tc.tile_pool(
        name="stage", bufs=4
    ) as stage, tc.tile_pool(name="work", bufs=4) as work, tc.psum_pool(
        name="flip", bufs=4
    ) as flip, tc.psum_pool(name="sums", bufs=4) as sums, tc.manual_schedule():
        forget_in = [
            keep.tile([P, SOURCES, TWINS, MEM], BF16, name="forget_in%d" % a)
            for a in range(PAIRS)
        ]
        x_codes = keep.tile([P, PAIRS, TWINS, SOURCES, PASSES * P], U32, align_bytes=64)
        x_scales = keep.tile([P, PAIRS, TWINS, SOURCES, PASSES * P], U8, align_bytes=64)
        w_codes = keep.tile([P, N_TILES, SOURCES * PASSES, 2 * N_TILE], U8, align_bytes=64)
        w_scales = [
            keep.tile([P, SOURCES * PASSES, N_TILE], U8, align_bytes=64, name="w_scales%d" % h)
            for h in range(N_TILES)
        ]
        identity = keep.tile([P, P], F32)
        ones = keep.tile([P, P], BF16)
        bias_rows = keep.tile([P, MEM], BF16)
        bias_all = keep.tile([P, MEM], F32)
        table_warm = keep.tile([P, 1], F32)
        clock_warm = keep.tile([P, N_TILE], BF16)

        nc.gpsimd.memset(clock_warm[:].bitcast(F32), 0.0)
        for h in range(N_TILES):
            nc.vector.memset(w_scales[h][:].bitcast(I32), 0)
        nc.vector.memset(bias_rows[:], 0.0)
        nc.vector.memset(ones[:], 1.0)
        nc.vector.memset(table_warm[:], 0.0)
        make_identity(nc, identity[:])
        nc.scalar.activation(out=table_warm[:], in_=table_warm[:], func=SIGMOID)

        def load_pair(a):
            for s in range(SOURCES):
                if a == PAIRS - 1 and s == SOURCES - 1:
                    for t in range(TWINS):
                        nc.sync.dma_start(
                            out=forget_in[a][:, s, t, :], in_=sources[s][a][:, t, :]
                        )
                else:
                    nc.sync.dma_start(out=forget_in[a][:, s, :, :], in_=sources[s][a])

        load_pair(0)
        scale_rows = fg_w_scales.rearrange("g (q r) n -> r q g n", r=4)

        def load_w_scales(h):
            cols = slice(h * N_TILE, (h + 1) * N_TILE)
            for r in range(4):
                nc.sync.dma_start(
                    out=w_scales[h][r:P:32, :, :].bitcast(I32),
                    in_=scale_rows[r][:, :, cols].bitcast(I32),
                )

        load_w_scales(0)
        nc.sync.dma_start(out=bias_rows[0:1, :], in_=fg_b.rearrange("(o n) -> o n", o=1))
        load_pair(1)
        def load_w_codes(h, first_pass, passes):
            nc.sync.dma_start(
                out=w_codes[:, h, first_pass : first_pass + passes, :].bitcast(I32),
                in_=fg_w_words[
                    first_pass : first_pass + passes, :, h * 2 * N_TILE : (h + 1) * 2 * N_TILE
                ]
                .rearrange("g p c -> p g c")
                .bitcast(I32),
            )

        for s in range(SOURCES):
            load_w_codes(0, s * PASSES, PASSES)
        load_w_scales(1)
        load_w_codes(1, 0, SOURCES * PASSES)

        idle_sum = sums.tile([P, N_TILE], F32, tag="sum")

        def idle_product():
            nc.tensor.matmul(
                out=idle_sum[:], lhsT=clock_warm[:, 0:P], rhs=clock_warm[:], start=True, stop=True
            )

        def spread_bias(h):
            cols = slice(h * N_TILE, (h + 1) * N_TILE)
            bias_sum = sums.tile([P, N_TILE], F32, tag="sum")
            nc.tensor.matmul(
                out=bias_sum[:], lhsT=ones[:], rhs=bias_rows[:, cols], start=True, stop=True
            )
            nc.scalar.copy(out=bias_all[:, cols], in_=bias_sum[:])

        for i in range(WARM_UPS):
            idle_product()

        for a in range(PAIRS):
            for s in range(SOURCES):
                grouped = []
                for t in range(TWINS):
                    words = forget_in[a][:, s, t, :].bitcast(F32)
                    flipped = flip.tile([P, PASSES, 2, P], F32, tag="flipped")
                    for g in range(PASSES):
                        for u in range(2):
                            nc.tensor.transpose(
                                flipped[:, g, u, :],
                                words[:, g * PASS_WORDS + u : (g + 1) * PASS_WORDS : 2],
                                identity[:],
                            )
                    side_by_side = stage.tile([P, PASSES * P * PACK], BF16, align_bytes=64)
                    copy = nc.scalar.copy if t % 2 == 0 else nc.vector.tensor_copy
                    copy(
                        out=side_by_side[:]
                        .bitcast(F32)
                        .rearrange("p (g b u) -> p g b u", g=PASSES, u=2),
                        in_=flipped[:].rearrange("p g u b -> p g b u"),
                    )
                    grouped.append(side_by_side)
                for t in range(TWINS):
                    nc.vector.quantize_mx(
                        out=x_codes[:, a, t, s, :].bitcast(FP8X4),
                        scales=x_scales[:, a, t, s, :],
                        in_=grouped[t][:],
                    )
                if a + s == 1:
                    spread_bias(a)

        def gate_of(h, a, t):
            cols = slice(h * N_TILE, (h + 1) * N_TILE)
            total = sums.tile([P, N_TILE], F32, tag="sum")
            for s in range(SOURCES):
                for g in range(PASSES):
                    batch = slice(g * P, (g + 1) * P)
                    nc.tensor.matmul_mx(
                        out=total[:],
                        lhsT=x_codes[:, a, t, s, batch].bitcast(FP8X4),
                        lhsT_scale=x_scales[:, a, t, s, batch],
                        rhs=w_codes[:, h, s * PASSES + g, :].bitcast(FP4X4),
                        rhs_scale=w_scales[h][:, s * PASSES + g, :],
                        start=(s == 0 and g == 0),
                        stop=(s == SOURCES - 1 and g == PASSES - 1),
                    )
            logit = work.tile([P, N_TILE], F32, tag="logit")
            nc.vector.tensor_tensor(out=logit[:], in0=total[:], in1=bias_all[:, cols], op=ADD)
            gate = work.tile([P, N_TILE], F32, tag="gate")
            nc.scalar.activation(out=gate[:], in_=logit[:], func=SIGMOID)
            return gate

        def store_gated(gate, h, a, t, engine):
            cols = slice(h * N_TILE, (h + 1) * N_TILE)
            result = work.tile([P, N_TILE], F32, tag="result")
            engine.tensor_tensor(
                out=result[:], in0=gate[:], in1=forget_in[a][:, 0, t, cols], op=MULT
            )
            nc.sync.dma_start(out=out_tiles[a][t][:, cols], in_=result[:])

        banks = [(h, a, t) for h in range(N_TILES) for a in range(PAIRS) for t in range(TWINS)]
        gates = []
        for j in range(len(banks) - 1):
            gates.append(gate_of(*banks[j]))
            if 0 < j < len(banks) - 2:
                store_gated(gates[j - 1], *banks[j - 1], nc.gpsimd if j % 2 == 1 else nc.vector)

        h_last, a_last, t_last = banks[-1]
        logit_last = work.tile([P, N_TILE], F32, tag="logit")
        gate_last = work.tile([P, N_TILE], F32, tag="gate")
        result_last = work.tile([P, N_TILE], F32, tag="result")

        def logit_of_group(c):
            inner = slice(c * N_GROUP, (c + 1) * N_GROUP)
            cols = slice(h_last * N_TILE + c * N_GROUP, h_last * N_TILE + (c + 1) * N_GROUP)
            bank = flip.tile([P, PASSES, 2, P], F32, tag="flipped")
            total = bank[:, 0, 0, :]
            for s in range(SOURCES):
                for g in range(PASSES):
                    batch = slice(g * P, (g + 1) * P)
                    nc.tensor.matmul_mx(
                        out=total,
                        lhsT=x_codes[:, a_last, t_last, s, batch].bitcast(FP8X4),
                        lhsT_scale=x_scales[:, a_last, t_last, s, batch],
                        rhs=w_codes[
                            :, h_last, s * PASSES + g, 2 * c * N_GROUP : 2 * (c + 1) * N_GROUP
                        ].bitcast(FP4X4),
                        rhs_scale=w_scales[h_last][:, s * PASSES + g, inner],
                        start=(s == 0 and g == 0),
                        stop=(s == SOURCES - 1 and g == PASSES - 1),
                    )
            nc.vector.tensor_tensor(
                out=logit_last[:, inner], in0=total, in1=bias_all[:, cols], op=ADD
            )

        def gate_of_half(d):
            inner = slice(d * 2 * N_GROUP, (d + 1) * 2 * N_GROUP)
            nc.scalar.activation(out=gate_last[:, inner], in_=logit_last[:, inner], func=SIGMOID)

        def store_gated_half(d):
            inner = slice(d * 2 * N_GROUP, (d + 1) * 2 * N_GROUP)
            cols = slice(h_last * N_TILE + d * 2 * N_GROUP, h_last * N_TILE + (d + 1) * 2 * N_GROUP)
            nc.vector.tensor_tensor(
                out=result_last[:, inner],
                in0=gate_last[:, inner],
                in1=forget_in[a_last][:, 0, t_last, cols],
                op=MULT,
            )
            nc.sync.dma_start(out=out_tiles[a_last][t_last][:, cols], in_=result_last[:, inner])

        logit_of_group(0)
        logit_of_group(1)
        gate_of_half(0)
        logit_of_group(2)
        logit_of_group(3)
        gate_of_half(1)
        store_gated(gates[-2], *banks[-3], nc.gpsimd)
        store_gated(gates[-1], *banks[-2], nc.vector)
        store_gated_half(0)
        store_gated_half(1)
